import numpy as np
import ml_dtypes


def mxq(x, axis, fmt="e4m3"):
    dtype, down = {"e4m3": (ml_dtypes.float8_e4m3fn, 7), "e5m2": (ml_dtypes.float8_e5m2, 14)}[fmt]
    v = np.moveaxis(np.asarray(x, np.float32).astype(ml_dtypes.bfloat16).astype(np.float64), axis, -1)
    blocks = v.reshape(v.shape[:-1] + (-1, 32))
    amax = np.abs(blocks).max(-1, keepdims=True)
    byte = np.maximum(np.where(amax > 0, np.frexp(amax)[1] - 1 + 127, 0) - down, 1)
    scale = np.exp2(byte - 127.0)
    codes = (blocks / scale).astype(np.float32).astype(dtype).astype(np.float64)
    return np.moveaxis((codes * scale).reshape(v.shape), -1, axis)


WIDE = False


def mx_kscale(k):
    if not WIDE:
        return np.ones(k)
    levels = np.array([10, -10, 5, -5, 0])
    a = np.random.permutation(np.resize(levels, k // 512 * 4)).reshape(k // 512, 4)
    idx = np.arange(k)
    return np.exp2(a[idx // 512, idx % 128 // 32])


BF16 = ml_dtypes.bfloat16


def bf(x):
    return np.asarray(x, np.float32).astype(BF16)


def f64(x):
    return np.asarray(x).astype(np.float64)


E2M1 = np.array([0.0, 0.5, 1.0, 1.5, 2.0, 3.0, 4.0, 6.0, -0.0, -0.5, -1.0, -1.5, -2.0, -3.0, -4.0, -6.0])


def pack_weight(w, fmt):
    k, n = w.shape
    w = f64(bf(w)).reshape(k // 32, 32, n)
    amax = np.abs(w).max(1)
    if fmt == "e4m3":
        byte = np.frexp(amax)[1] - 1 + 127 - 7
    else:
        mant, ex = np.frexp(amax / 6.0)
        byte = np.where(mant > 0.5, ex, ex - 1) + 127
    byte = np.clip(np.where(amax > 0, byte, 1), 1, 254)
    scaled = (w * np.exp2(127.0 - byte)[:, None, :]).reshape(k, n).astype(np.float32)
    by_word = np.ascontiguousarray(scaled.reshape(k // 512, 128, 4, n).transpose(0, 1, 3, 2))
    if fmt == "e4m3":
        words = by_word.astype(ml_dtypes.float8_e4m3fn).view(np.uint8)
    else:
        c = by_word.astype(ml_dtypes.float4_e2m1fn).view(np.uint8) & 0xF
        words = c[..., 0::2] | (c[..., 1::2] << 4)
    return np.ascontiguousarray(words), np.ascontiguousarray(byte.astype(np.uint8).reshape(k // 512, 16, n))


def unpack_weight(words, scales, fmt):
    g, p, n, _ = words.shape
    if fmt == "e4m3":
        vals = np.ascontiguousarray(words).view(ml_dtypes.float8_e4m3fn).astype(np.float64)
    else:
        nib = np.empty((g, p, n, 4), np.uint8)
        nib[..., 0::2] = words & 0xF
        nib[..., 1::2] = words >> 4
        vals = E2M1[nib]
    vals = vals * np.repeat(np.exp2(scales.astype(np.float64) - 127.0), 8, axis=1)[..., None]
    return vals.transpose(0, 1, 3, 2).reshape(g * 512, n)


B, L, S, D, H = 12, 384, 128, 512, 4
HD = D // H
T = S + L


def to_mha(t):
    return t.reshape(t.shape[0], t.shape[1], H, HD).transpose(0, 2, 1, 3)


def setup_inputs():
    s = mx_kscale(D)
    q_rot = bf(np.random.standard_normal((B, H, T, HD)))
    k_rot = bf(np.random.standard_normal((B, H, T, HD)))
    x = bf(np.random.standard_normal((B, L, D)) * s)
    c = bf(np.random.standard_normal((B, S, D)) * s)
    Wv_x_words, Wv_x_scales = pack_weight(np.random.standard_normal((D, D)) * 3.0 / np.sqrt(D) / s[:, None], "e4m3")
    bv_x = bf(np.random.standard_normal(D) * 0.2)
    Wv_c_words, Wv_c_scales = pack_weight(np.random.standard_normal((D, D)) * 3.0 / np.sqrt(D) / s[:, None], "e4m3")
    bv_c = bf(np.random.standard_normal(D) * 0.2)
    return {
        "q_rot": q_rot,
        "k_rot": k_rot,
        "x": x,
        "c": c,
        "Wv_x_words": Wv_x_words,
        "Wv_x_scales": Wv_x_scales,
        "bv_x": bv_x,
        "Wv_c_words": Wv_c_words,
        "Wv_c_scales": Wv_c_scales,
        "bv_c": bv_c,
    }


def reference(q_rot, k_rot, x, c, Wv_x_words, Wv_x_scales, bv_x, Wv_c_words, Wv_c_scales, bv_c):
    vc = to_mha((mxq(f64(c), 2, "e4m3") @ unpack_weight(Wv_c_words, Wv_c_scales, "e4m3")) + f64(bv_c))
    vx = to_mha((mxq(f64(x), 2, "e4m3") @ unpack_weight(Wv_x_words, Wv_x_scales, "e4m3")) + f64(bv_x))
    v = np.concatenate([vc, vx], axis=2)
    scores = f64(q_rot) @ f64(k_rot).transpose(0, 1, 3, 2) / np.sqrt(HD)
    e = np.exp(scores - scores.max(-1, keepdims=True))
    y = (mxq(e, 3, "e4m3") @ mxq(v, 2, "e4m3")) / e.sum(-1, keepdims=True)
    y = y.transpose(0, 2, 1, 3).reshape(B, T, D)
    return y[:, S:], y[:, :S]

@@ -1,0 +1,376 @@
+import math
+from contextlib import ExitStack
+
+import concourse.mybir as mybir
+from concourse.masks import make_identity
+
+F32 = mybir.dt.float32
+BF16 = mybir.dt.bfloat16
+U32 = mybir.dt.uint32
+U8 = mybir.dt.uint8
+I32 = mybir.dt.int32
+FP8X4 = mybir.dt.float8_e4m3fn_x4
+
+P = 128
+PACK = 4
+BATCH = 12
+HEADS_PER_ITEM = 4
+SEQ = 512
+HEAD_DIM = 128
+MODEL_DIM = 512
+TILES = SEQ // P
+HEADS = BATCH * HEADS_PER_ITEM
+UNITS = HEADS * TILES
+PAIRS = UNITS // 2
+TOKEN_TILES = BATCH * TILES
+SCALE = 1.0 / math.sqrt(HEAD_DIM)
+
+FLOPS = 3 * 2 * BATCH * SEQ * SEQ * MODEL_DIM
+
+TOKEN_LEAD = 5
+FIRST_STEP = -2 * TOKEN_LEAD
+LAST_STEP = PAIRS + 2
+STEPS_PER_ITEM = 2 * HEADS_PER_ITEM
+
+
+def tile_dualstreamattentionwithrotaryembedding_pb_t_kernel(
+    tc, q_rot, k_rot, x, c, Wv_x_words, Wv_x_scales, bv_x, Wv_c_words, Wv_c_scales, bv_c, out_0, out_1
+):
+    nc = tc.nc
+    with ExitStack() as ctx:
+        ctx.enter_context(tc.manual_schedule())
+        const = ctx.enter_context(tc.tile_pool(name="const", bufs=1))
+        stream = ctx.enter_context(tc.tile_pool(name="stream", bufs=3))
+        work = ctx.enter_context(tc.tile_pool(name="work", bufs=3))
+        psum_scores = ctx.enter_context(tc.psum_pool(name="psum_scores", bufs=4))
+        psum_turned = ctx.enter_context(tc.psum_pool(name="psum_turned", bufs=2))
+        psum_mx = ctx.enter_context(tc.psum_pool(name="psum_mx", bufs=1))
+
+        held = {}
+
+        ident_bf16 = const.tile([P, P], BF16, name="ident_bf16")
+        make_identity(nc, ident_bf16[:])
+        ident_f32 = const.tile([P, P], F32, name="ident_f32")
+        make_identity(nc, ident_f32[:])
+
+        w_codes = const.tile([P, 2, MODEL_DIM], U32, name="w_codes", align_bytes=64)
+        w_scales = const.tile([P, 2, MODEL_DIM], U8, name="w_scales", align_bytes=64)
+        nc.vector.memset(w_scales[:].rearrange("p s n -> p (s n)").bitcast(I32), 0)
+        bias = const.tile([P, TILES, MODEL_DIM], BF16, name="bias")
+
+        def load_weights():
+            given = ((Wv_c_words, Wv_c_scales), (Wv_x_words, Wv_x_scales))
+            for s, (words, scales) in enumerate(given):
+                nc.sync.dma_start(
+                    out=w_codes[:, s, :].bitcast(I32),
+                    in_=words[0].rearrange("p n t -> p (n t)").bitcast(I32),
+                )
+                for quadrant in range(4):
+                    nc.sync.dma_start(
+                        out=w_scales[32 * quadrant : 32 * quadrant + 4, s, :].bitcast(I32),
+                        in_=scales[0, 4 * quadrant : 4 * quadrant + 4, :].bitcast(I32),
+                    )
+            nc.sync.dma_start(out=bias[:, 0, :], in_=bv_c.partition_broadcast(P))
+            nc.sync.dma_start(out=bias[:, 1, :], in_=bv_x.partition_broadcast(P))
+            nc.gpsimd.tensor_copy(
+                out=bias[:, 2:TILES, :], in_=bias[:, 1:2, :].to_broadcast([P, TILES - 2, MODEL_DIM])
+            )
+
+        def load_tokens(item):
+            if not 0 <= item < BATCH:
+                return
+            tokens = stream.tile([P, TILES, MODEL_DIM], BF16, name="tokens")
+            nc.sync.dma_start(out=tokens[:, 0, :], in_=c[item])
+            nc.sync.dma_start(
+                out=tokens[:, 1:TILES, :], in_=x[item].rearrange("(t p) k -> p t k", p=P)
+            )
+            held["tokens", item] = tokens
+
+        def load_queries_and_keys(item):
+            if not 0 <= item < BATCH:
+                return
+            queries = stream.tile([P, HEADS_PER_ITEM * TILES, HEAD_DIM], BF16, name="queries")
+            nc.sync.dma_start(out=queries[:], in_=q_rot[item].rearrange("h (t p) d -> p (h t) d", p=P))
+            keys = stream.tile([P, HEADS_PER_ITEM * TILES, HEAD_DIM], BF16, name="keys")
+            nc.sync.dma_start(out=keys[:], in_=k_rot[item].rearrange("h (t p) d -> p (h t) d", p=P))
+            held["queries", item] = queries
+            held["keys", item] = keys
+
+        def store(item):
+            if not 0 <= item < BATCH:
+                return
+            y_sb = held["y_sb", item]
+            nc.sync.dma_start(out=out_1[item], in_=y_sb[:, 0, :])
+            nc.sync.dma_start(
+                out=out_0[item].rearrange("(t p) n -> p t n", p=P), in_=y_sb[:, 1:TILES, :]
+            )
+
+        def transpose_tokens(tile_index):
+            if not 0 <= tile_index < TOKEN_TILES:
+                return
+            item, t = divmod(tile_index, TILES)
+            words = held["tokens", item][:, t, :].bitcast(F32)
+            turned = psum_turned.tile([P, 2, P], F32, name="tokens_turned", tag="turned")
+            for u in range(2):
+                nc.tensor.transpose(turned[:, u, :], words[:, u : MODEL_DIM // 2 : 2], ident_f32[:])
+            held["tokens_turned", tile_index] = turned
+
+        def regroup_tokens(tile_index):
+            if not 0 <= tile_index < TOKEN_TILES:
+                return
+            grouped = work.tile([P, P, PACK], BF16, name="tokens_grouped", align_bytes=64)
+            nc.scalar.copy(
+                out=grouped[:].bitcast(F32),
+                in_=held["tokens_turned", tile_index][:].rearrange("p u i -> p i u"),
+            )
+            held["tokens_grouped", tile_index] = grouped
+
+        def quantise_tokens(tile_index):
+            if not 0 <= tile_index < TOKEN_TILES:
+                return
+            item, t = divmod(tile_index, TILES)
+            if t == 0:
+                held["x_codes", item] = work.tile([P, SEQ], U32, name="x_codes", align_bytes=64)
+                held["x_scales", item] = work.tile([P, SEQ], U8, name="x_scales", align_bytes=64)
+            columns = slice(t * P, (t + 1) * P)
+            nc.vector.quantize_mx(
+                out=held["x_codes", item][:, columns].bitcast(FP8X4),
+                scales=held["x_scales", item][:, columns],
+                in_=held["tokens_grouped", tile_index][:].rearrange("p i t -> p (i t)"),
+            )
+
+        def project_values(head):
+            if not 0 <= head < HEADS:
+                return
+            item, h = divmod(head, HEADS_PER_ITEM)
+            v_ps = psum_mx.tile([P, TILES, HEAD_DIM], F32, name="v_ps")
+            for t in range(TILES):
+                s = min(t, 1)
+                nc.tensor.matmul_mx(
+                    out=v_ps[:, t, :],
+                    lhsT=held["x_codes", item][:, t * P : (t + 1) * P].bitcast(FP8X4),
+                    lhsT_scale=held["x_scales", item][:, t * P : (t + 1) * P],
+                    rhs=w_codes[:, s, h * HEAD_DIM : (h + 1) * HEAD_DIM].bitcast(FP8X4),
+                    rhs_scale=w_scales[:, s, h * HEAD_DIM : (h + 1) * HEAD_DIM],
+                    start=True,
+                    stop=True,
+                )
+            held["v_ps", head] = v_ps
+
+        def add_bias(head):
+            if not 0 <= head < HEADS:
+                return
+            h = head % HEADS_PER_ITEM
+            grouped = work.tile([P, HEAD_DIM, PACK], BF16, name="v_grouped", align_bytes=64)
+            nc.vector.tensor_tensor(
+                out=grouped[:],
+                in0=held["v_ps", head][:].rearrange("p t d -> p d t"),
+                in1=bias[:, :, h * HEAD_DIM : (h + 1) * HEAD_DIM].rearrange("p t d -> p d t"),
+                op=mybir.AluOpType.add,
+            )
+            held["v_grouped", head] = grouped
+
+        def quantise_values(head):
+            if not 0 <= head < HEADS:
+                return
+            v_codes = work.tile([P, HEAD_DIM], U32, name="v_codes", align_bytes=64)
+            v_scales = work.tile([P, HEAD_DIM], U8, name="v_scales", align_bytes=64)
+            nc.vector.quantize_mx(
+                out=v_codes[:].bitcast(FP8X4),
+                scales=v_scales[:],
+                in_=held["v_grouped", head][:].rearrange("p d t -> p (d t)"),
+            )
+            held["v_codes", head] = v_codes
+            held["v_scales", head] = v_scales
+
+        def transpose_queries_and_keys(head):
+            if not 0 <= head < HEADS:
+                return
+            item, h = divmod(head, HEADS_PER_ITEM)
+            turned = psum_turned.tile([P, 2, SEQ], BF16, name="qk_turned", tag="turned")
+            for side, name in enumerate(("queries", "keys")):
+                for t in range(TILES):
+                    nc.tensor.transpose(
+                        turned[:, side, t * P : (t + 1) * P],
+                        held[name, item][:, h * TILES + t, :],
+                        ident_bf16[:],
+                    )
+            held["qk_turned", head] = turned
+
+        def copy_queries_and_keys(head):
+            if not 0 <= head < HEADS:
+                return
+            qk = work.tile([P, 2, SEQ], BF16, name="qk")
+            nc.scalar.copy(out=qk[:], in_=held["qk_turned", head][:])
+            held["qk", head] = qk
+
+        def scores(unit):
+            if not 0 <= unit < UNITS:
+                return
+            head, i = divmod(unit, TILES)
+            s_ps = psum_scores.tile([P, SEQ], F32, name="s_ps")
+            nc.tensor.matmul(
+                out=s_ps[:],
+                lhsT=held["qk", head][:, 0, i * P : (i + 1) * P],
+                rhs=held["qk", head][:, 1, :],
+                start=True,
+                stop=True,
+            )
+            held["s_ps", unit] = s_ps
+
+        def row_max(unit):
+            if not 0 <= unit < UNITS:
+                return
+            pair, a = divmod(unit, 2)
+            if a == 0:
+                held["row_max", pair] = work.tile([P, 2], F32, name="row_max")
+            nc.vector.tensor_reduce(
+                out=held["row_max", pair][:, a : a + 1],
+                in_=held["s_ps", unit][:],
+                axis=mybir.AxisListType.X,
+                op=mybir.AluOpType.max,
+            )
+
+        def shift_of(pair):
+            if not 0 <= pair < PAIRS:
+                return
+            shift = work.tile([P, 2], F32, name="shift")
+            nc.vector.tensor_scalar_mul(out=shift[:], in0=held["row_max", pair][:], scalar1=-SCALE)
+            held["shift", pair] = shift
+
+        def exponentials(unit):
+            if not 0 <= unit < UNITS:
+                return
+            pair, a = divmod(unit, 2)
+            head, i = divmod(unit, TILES)
+            if a == 0:
+                held["e", pair] = work.tile([P, 2, SEQ], BF16, name="e")
+            if i == 0:
+                held["row_sum", head] = work.tile([P, TILES], F32, name="row_sum")
+            nc.scalar.activation(
+                out=held["e", pair][:, a, :].rearrange("q (u p j) -> q u p j", u=2, j=2),
+                in_=held["s_ps", unit][:].rearrange("q (u j p) -> q u p j", u=2, j=2),
+                func=mybir.ActivationFunctionType.Exp,
+                bias=held["shift", pair][:, a : a + 1],
+                scale=SCALE,
+                accum_out=held["row_sum", head][:, i : i + 1],
+            )
+
+        def transpose_e(pair):
+            if not 0 <= pair < PAIRS:
+                return
+            turned = psum_turned.tile([P, 2, 2, P], F32, name="e_turned", tag="turned")
+            for a in range(2):
+                words = held["e", pair][:, a, :].bitcast(F32)
+                for u in range(2):
+                    nc.tensor.transpose(turned[:, a, u, :], words[:, u * P : (u + 1) * P], ident_f32[:])
+            held["e_turned", pair] = turned
+
+        def regroup_e(pair):
+            if not 0 <= pair < PAIRS:
+                return
+            grouped = work.tile([P, 2, P, PACK], BF16, name="e_grouped", align_bytes=64)
+            nc.scalar.copy(
+                out=grouped[:].bitcast(F32),
+                in_=held["e_turned", pair][:].rearrange("p a u q -> p a q u"),
+            )
+            held["e_grouped", pair] = grouped
+
+        def quantise_e(pair):
+            if not 0 <= pair < PAIRS:
+                return
+            e_codes = work.tile([P, 2 * P], U32, name="e_codes", align_bytes=64)
+            e_scales = work.tile([P, 2 * P], U8, name="e_scales", align_bytes=64)
+            nc.vector.quantize_mx(
+                out=e_codes[:].bitcast(FP8X4),
+                scales=e_scales[:],
+                in_=held["e_grouped", pair][:].rearrange("p a q t -> p (a q t)"),
+            )
+            held["e_codes", pair] = e_codes
+            held["e_scales", pair] = e_scales
+
+        def attend(pair):
+            if not 0 <= pair < PAIRS:
+                return
+            head, half = divmod(pair, 2)
+            if half == 0:
+                held["y_ps", head] = psum_mx.tile([P, TILES, HEAD_DIM], F32, name="y_ps")
+            for a in range(2):
+                nc.tensor.matmul_mx(
+                    out=held["y_ps", head][:, 2 * half + a, :],
+                    lhsT=held["e_codes", pair][:, a * P : (a + 1) * P].bitcast(FP8X4),
+                    lhsT_scale=held["e_scales", pair][:, a * P : (a + 1) * P],
+                    rhs=held["v_codes", head][:].bitcast(FP8X4),
+                    rhs_scale=held["v_scales", head][:],
+                    start=True,
+                    stop=True,
+                )
+
+        def reciprocal_of_row_sums(head):
+            if not 0 <= head < HEADS:
+                return
+            inverse = work.tile([P, TILES], F32, name="inverse")
+            nc.vector.reciprocal(out=inverse[:], in_=held["row_sum", head][:])
+            held["inverse", head] = inverse
+
+        def normalise(head):
+            if not 0 <= head < HEADS:
+                return
+            item, h = divmod(head, HEADS_PER_ITEM)
+            if h == 0:
+                held["y_sb", item] = stream.tile([P, TILES, MODEL_DIM], F32, name="y_sb")
+            nc.vector.tensor_tensor(
+                out=held["y_sb", item][:, :, h * HEAD_DIM : (h + 1) * HEAD_DIM],
+                in0=held["y_ps", head][:],
+                in1=held["inverse", head][:].unsqueeze(2).to_broadcast([P, TILES, HEAD_DIM]),
+                op=mybir.AluOpType.mult,
+            )
+
+        load_tokens(0)
+        load_queries_and_keys(0)
+        load_weights()
+        load_tokens(1)
+        load_queries_and_keys(1)
+        load_tokens(2)
+
+        for step in range(FIRST_STEP, LAST_STEP + 1):
+            even = step % 2 == 0
+            half = step // 2
+
+            scores(2 * step + 2)
+            attend(step - 3)
+            if even:
+                project_values(half)
+            scores(2 * step + 3)
+            transpose_e(step - 1)
+            if even:
+                transpose_tokens(half + TOKEN_LEAD)
+            else:
+                transpose_queries_and_keys(half + 2)
+
+            exponentials(2 * step)
+            exponentials(2 * step + 1)
+            regroup_e(step - 1)
+            if even:
+                regroup_tokens(half + TOKEN_LEAD)
+            else:
+                copy_queries_and_keys(half + 2)
+
+            if even:
+                normalise(half - 2)
+            row_max(2 * step + 2)
+            row_max(2 * step + 3)
+            quantise_e(step - 2)
+            shift_of(step + 1)
+            if even:
+                add_bias(half)
+            else:
+                quantise_values(half)
+                quantise_tokens(half + TOKEN_LEAD)
+                reciprocal_of_row_sums(half - 1)
+
+            if step % STEPS_PER_ITEM == 2:
+                store((step - 10) // STEPS_PER_ITEM)
+            if step % STEPS_PER_ITEM == 5:
+                load_queries_and_keys((step + 3) // STEPS_PER_ITEM + 2)
+                load_tokens((step + 3) // STEPS_PER_ITEM + 3)

@@ -338,15 +338,15 @@ def tile_dualstreamattentionwithrotaryembedding_pb_t_kernel(
             half = step // 2
 
             scores(2 * step + 2)
-            attend(step - 3)
-            if even:
-                project_values(half)
             scores(2 * step + 3)
             transpose_e(step - 1)
             if even:
                 transpose_tokens(half + TOKEN_LEAD)
             else:
                 transpose_queries_and_keys(half + 2)
+            attend(step - 3)
+            if even:
+                project_values(half)
 
             exponentials(2 * step)
             exponentials(2 * step + 1)
@@ -356,13 +356,12 @@ def tile_dualstreamattentionwithrotaryembedding_pb_t_kernel(
             else:
                 copy_queries_and_keys(half + 2)
 
-            if even:
-                normalise(half - 2)
             row_max(2 * step + 2)
             row_max(2 * step + 3)
             quantise_e(step - 2)
             shift_of(step + 1)
             if even:
+                normalise(half - 2)
                 add_bias(half)
             else:
                 quantise_values(half)

@@ -27,9 +27,9 @@ SCALE = 1.0 / math.sqrt(HEAD_DIM)
 
 FLOPS = 3 * 2 * BATCH * SEQ * SEQ * MODEL_DIM
 
-TOKEN_LEAD = 5
-FIRST_STEP = -2 * TOKEN_LEAD
-LAST_STEP = PAIRS + 2
+TOKEN_LEAD = TILES - 1
+ATTEND_LAG = 5
+LAST_STEP = PAIRS - 1 + ATTEND_LAG
 STEPS_PER_ITEM = 2 * HEADS_PER_ITEM
 
 
@@ -70,9 +70,13 @@ def tile_dualstreamattentionwithrotaryembedding_pb_t_kernel(
                         out=w_scales[32 * quadrant : 32 * quadrant + 4, s, :].bitcast(I32),
                         in_=scales[0, 4 * quadrant : 4 * quadrant + 4, :].bitcast(I32),
                     )
+
+        def load_biases():
             nc.sync.dma_start(out=bias[:, 0, :], in_=bv_c.partition_broadcast(P))
             nc.sync.dma_start(out=bias[:, 1, :], in_=bv_x.partition_broadcast(P))
-            nc.gpsimd.tensor_copy(
+
+        def repeat_bias_of_x():
+            nc.scalar.copy(
                 out=bias[:, 2:TILES, :], in_=bias[:, 1:2, :].to_broadcast([P, TILES - 2, MODEL_DIM])
             )
 
@@ -86,15 +90,21 @@ def tile_dualstreamattentionwithrotaryembedding_pb_t_kernel(
             )
             held["tokens", item] = tokens
 
-        def load_queries_and_keys(item):
+        def load_queries_and_keys(item, first_head=0, last_head=HEADS_PER_ITEM - 1):
             if not 0 <= item < BATCH:
                 return
-            queries = stream.tile([P, HEADS_PER_ITEM * TILES, HEAD_DIM], BF16, name="queries")
-            nc.sync.dma_start(out=queries[:], in_=q_rot[item].rearrange("h (t p) d -> p (h t) d", p=P))
-            keys = stream.tile([P, HEADS_PER_ITEM * TILES, HEAD_DIM], BF16, name="keys")
-            nc.sync.dma_start(out=keys[:], in_=k_rot[item].rearrange("h (t p) d -> p (h t) d", p=P))
-            held["queries", item] = queries
-            held["keys", item] = keys
+            if first_head == 0:
+                for name in ("queries", "keys"):
+                    held[name, item] = stream.tile(
+                        [P, HEADS_PER_ITEM * TILES, HEAD_DIM], BF16, name=name
+                    )
+            heads = slice(first_head, last_head + 1)
+            rows = slice(first_head * TILES, (last_head + 1) * TILES)
+            for name, source in (("queries", q_rot), ("keys", k_rot)):
+                nc.sync.dma_start(
+                    out=held[name, item][:, rows, :],
+                    in_=source[item, heads].rearrange("h (t p) d -> p (h t) d", p=P),
+                )
 
         def store(item):
             if not 0 <= item < BATCH:
@@ -279,8 +289,8 @@ def tile_dualstreamattentionwithrotaryembedding_pb_t_kernel(
         def quantise_e(pair):
             if not 0 <= pair < PAIRS:
                 return
-            e_codes = work.tile([P, 2 * P], U32, name="e_codes", align_bytes=64)
-            e_scales = work.tile([P, 2 * P], U8, name="e_scales", align_bytes=64)
+            e_codes = work.tile([P, 2 * P], U32, name="e_codes", align_bytes=64, bufs=ATTEND_LAG)
+            e_scales = work.tile([P, 2 * P], U8, name="e_scales", align_bytes=64, bufs=ATTEND_LAG)
             nc.vector.quantize_mx(
                 out=e_codes[:].bitcast(FP8X4),
                 scales=e_scales[:],
@@ -326,14 +336,32 @@ def tile_dualstreamattentionwithrotaryembedding_pb_t_kernel(
                 op=mybir.AluOpType.mult,
             )
 
+        load_queries_and_keys(0, 0, 0)
         load_tokens(0)
-        load_queries_and_keys(0)
+        load_queries_and_keys(0, 1, 1)
         load_weights()
+        load_queries_and_keys(0, 2, 3)
+        load_biases()
         load_tokens(1)
         load_queries_and_keys(1)
         load_tokens(2)
+        load_queries_and_keys(2)
 
-        for step in range(FIRST_STEP, LAST_STEP + 1):
+        transpose_queries_and_keys(0)
+        copy_queries_and_keys(0)
+        scores(0)
+        scores(1)
+        row_max(0)
+        row_max(1)
+        shift_of(0)
+        for tile_index in range(TOKEN_LEAD):
+            transpose_tokens(tile_index)
+            regroup_tokens(tile_index)
+            quantise_tokens(tile_index)
+        transpose_queries_and_keys(1)
+        copy_queries_and_keys(1)
+
+        for step in range(LAST_STEP + 1):
             even = step % 2 == 0
             half = step // 2
 
@@ -344,9 +372,9 @@ def tile_dualstreamattentionwithrotaryembedding_pb_t_kernel(
                 transpose_tokens(half + TOKEN_LEAD)
             else:
                 transpose_queries_and_keys(half + 2)
-            attend(step - 3)
+            attend(step - ATTEND_LAG)
             if even:
-                project_values(half)
+                project_values(half - 1)
 
             exponentials(2 * step)
             exponentials(2 * step + 1)
@@ -355,21 +383,24 @@ def tile_dualstreamattentionwithrotaryembedding_pb_t_kernel(
                 regroup_tokens(half + TOKEN_LEAD)
             else:
                 copy_queries_and_keys(half + 2)
+            if step == 1:
+                repeat_bias_of_x()
 
             row_max(2 * step + 2)
             row_max(2 * step + 3)
             quantise_e(step - 2)
             shift_of(step + 1)
             if even:
-                normalise(half - 2)
-                add_bias(half)
+                normalise(half - 3)
+                add_bias(half - 1)
             else:
-                quantise_values(half)
+                quantise_values(half - 1)
                 quantise_tokens(half + TOKEN_LEAD)
                 reciprocal_of_row_sums(half - 1)
 
-            if step % STEPS_PER_ITEM == 2:
-                store((step - 10) // STEPS_PER_ITEM)
+            if step % STEPS_PER_ITEM == 4:
+                store((step - 12) // STEPS_PER_ITEM)
+            if step % STEPS_PER_ITEM == 1:
+                load_tokens(step // STEPS_PER_ITEM + 3)
             if step % STEPS_PER_ITEM == 5:
-                load_queries_and_keys((step + 3) // STEPS_PER_ITEM + 2)
-                load_tokens((step + 3) // STEPS_PER_ITEM + 3)
+                load_queries_and_keys(step // STEPS_PER_ITEM + 3)

@@ -245,7 +245,14 @@ def tile_dualstreamattentionwithrotaryembedding_pb_t_kernel(
             if not 0 <= pair < PAIRS:
                 return
             shift = work.tile([P, 2], F32, name="shift")
-            nc.vector.tensor_scalar_mul(out=shift[:], in0=held["row_max", pair][:], scalar1=-SCALE)
+            nc.gpsimd.tensor_scalar(
+                out=shift[:],
+                in0=held["row_max", pair][:],
+                scalar1=-SCALE,
+                scalar2=0.0,
+                op0=mybir.AluOpType.mult,
+                op1=mybir.AluOpType.add,
+            )
             held["shift", pair] = shift
 
         def exponentials(unit):
@@ -388,8 +395,8 @@ def tile_dualstreamattentionwithrotaryembedding_pb_t_kernel(
 
             row_max(2 * step + 2)
             row_max(2 * step + 3)
-            quantise_e(step - 2)
             shift_of(step + 1)
+            quantise_e(step - 2)
             if even:
                 normalise(half - 3)
                 add_bias(half - 1)

@@ -86,7 +86,7 @@ def tile_dualstreamattentionwithrotaryembedding_pb_t_kernel(
             tokens = stream.tile([P, TILES, MODEL_DIM], BF16, name="tokens")
             nc.sync.dma_start(out=tokens[:, 0, :], in_=c[item])
             nc.sync.dma_start(
-                out=tokens[:, 1:TILES, :], in_=x[item].rearrange("(t p) k -> p t k", p=P)
+                out=tokens[:, 1:TILES, :], in_=x[item].rearrange("(p t) k -> p t k", p=P)
             )
             held["tokens", item] = tokens
 
@@ -99,11 +99,15 @@ def tile_dualstreamattentionwithrotaryembedding_pb_t_kernel(
                         [P, HEADS_PER_ITEM * TILES, HEAD_DIM], BF16, name=name
                     )
             heads = slice(first_head, last_head + 1)
-            rows = slice(first_head * TILES, (last_head + 1) * TILES)
             for name, source in (("queries", q_rot), ("keys", k_rot)):
+                tile = held[name, item][:].rearrange("p (h t) d -> p h (t d)", t=TILES)
                 nc.sync.dma_start(
-                    out=held[name, item][:, rows, :],
-                    in_=source[item, heads].rearrange("h (t p) d -> p (h t) d", p=P),
+                    out=tile[:, heads, 0:HEAD_DIM],
+                    in_=source[item, heads, 0:P, :].rearrange("h p d -> p h d"),
+                )
+                nc.sync.dma_start(
+                    out=tile[:, heads, HEAD_DIM:],
+                    in_=source[item, heads, P:SEQ, :].rearrange("h (p t) d -> p h (t d)", p=P),
                 )
 
         def store(item):
@@ -112,7 +116,7 @@ def tile_dualstreamattentionwithrotaryembedding_pb_t_kernel(
             y_sb = held["y_sb", item]
             nc.sync.dma_start(out=out_1[item], in_=y_sb[:, 0, :])
             nc.sync.dma_start(
-                out=out_0[item].rearrange("(t p) n -> p t n", p=P), in_=y_sb[:, 1:TILES, :]
+                out=out_0[item].rearrange("(p t) n -> p t n", p=P), in_=y_sb[:, 1:TILES, :]
             )
 
         def transpose_tokens(tile_index):

@@ -29,7 +29,6 @@ FLOPS = 3 * 2 * BATCH * SEQ * SEQ * MODEL_DIM
 
 TOKEN_LEAD = TILES - 1
 ATTEND_LAG = 5
-LAST_STEP = PAIRS - 1 + ATTEND_LAG
 STEPS_PER_ITEM = 2 * HEADS_PER_ITEM
 
 
@@ -56,7 +55,8 @@ def tile_dualstreamattentionwithrotaryembedding_pb_t_kernel(
         w_codes = const.tile([P, 2, MODEL_DIM], U32, name="w_codes", align_bytes=64)
         w_scales = const.tile([P, 2, MODEL_DIM], U8, name="w_scales", align_bytes=64)
         nc.vector.memset(w_scales[:].rearrange("p s n -> p (s n)").bitcast(I32), 0)
-        bias = const.tile([P, TILES, MODEL_DIM], BF16, name="bias")
+        bias = const.tile([P, MODEL_DIM, TILES], BF16, name="bias")
+        bias_rows = const.tile([P, TILES, MODEL_DIM], BF16, name="bias_rows")
 
         def load_weights():
             given = ((Wv_c_words, Wv_c_scales), (Wv_x_words, Wv_x_scales))
@@ -72,13 +72,15 @@ def tile_dualstreamattentionwithrotaryembedding_pb_t_kernel(
                     )
 
         def load_biases():
-            nc.sync.dma_start(out=bias[:, 0, :], in_=bv_c.partition_broadcast(P))
-            nc.sync.dma_start(out=bias[:, 1, :], in_=bv_x.partition_broadcast(P))
+            nc.sync.dma_start(out=bias_rows[:, 0, :], in_=bv_c.partition_broadcast(P))
+            nc.sync.dma_start(out=bias_rows[:, 1, :], in_=bv_x.partition_broadcast(P))
 
-        def repeat_bias_of_x():
-            nc.scalar.copy(
-                out=bias[:, 2:TILES, :], in_=bias[:, 1:2, :].to_broadcast([P, TILES - 2, MODEL_DIM])
+        def interleave_biases():
+            nc.vector.tensor_copy(
+                out=bias_rows[:, 2:TILES, :],
+                in_=bias_rows[:, 1:2, :].to_broadcast([P, TILES - 2, MODEL_DIM]),
             )
+            nc.vector.tensor_copy(out=bias[:], in_=bias_rows[:].rearrange("p t n -> p n t"))
 
         def load_tokens(item):
             if not 0 <= item < BATCH:
@@ -110,13 +112,17 @@ def tile_dualstreamattentionwithrotaryembedding_pb_t_kernel(
                     in_=source[item, heads, P:SEQ, :].rearrange("h (p t) d -> p h (t d)", p=P),
                 )
 
-        def store(item):
+        def store(item, heads=(0, HEADS_PER_ITEM), tiles=(0, TILES)):
             if not 0 <= item < BATCH:
                 return
             y_sb = held["y_sb", item]
-            nc.sync.dma_start(out=out_1[item], in_=y_sb[:, 0, :])
+            columns = slice(heads[0] * HEAD_DIM, heads[1] * HEAD_DIM)
+            if tiles[0] == 0:
+                nc.sync.dma_start(out=out_1[item, :, columns], in_=y_sb[:, 0, columns])
+            first = max(tiles[0], 1)
             nc.sync.dma_start(
-                out=out_0[item].rearrange("(p t) n -> p t n", p=P), in_=y_sb[:, 1:TILES, :]
+                out=out_0[item].rearrange("(p t) n -> p t n", p=P)[:, first - 1 : tiles[1] - 1, columns],
+                in_=y_sb[:, first : tiles[1], columns],
             )
 
         def transpose_tokens(tile_index):
@@ -129,11 +135,11 @@ def tile_dualstreamattentionwithrotaryembedding_pb_t_kernel(
                 nc.tensor.transpose(turned[:, u, :], words[:, u : MODEL_DIM // 2 : 2], ident_f32[:])
             held["tokens_turned", tile_index] = turned
 
-        def regroup_tokens(tile_index):
+        def regroup_tokens(tile_index, copy=nc.scalar.copy):
             if not 0 <= tile_index < TOKEN_TILES:
                 return
             grouped = work.tile([P, P, PACK], BF16, name="tokens_grouped", align_bytes=64)
-            nc.scalar.copy(
+            copy(
                 out=grouped[:].bitcast(F32),
                 in_=held["tokens_turned", tile_index][:].rearrange("p u i -> p i u"),
             )
@@ -179,7 +185,7 @@ def tile_dualstreamattentionwithrotaryembedding_pb_t_kernel(
             nc.vector.tensor_tensor(
                 out=grouped[:],
                 in0=held["v_ps", head][:].rearrange("p t d -> p d t"),
-                in1=bias[:, :, h * HEAD_DIM : (h + 1) * HEAD_DIM].rearrange("p t d -> p d t"),
+                in1=bias[:, h * HEAD_DIM : (h + 1) * HEAD_DIM, :],
                 op=mybir.AluOpType.add,
             )
             held["v_grouped", head] = grouped
@@ -211,11 +217,11 @@ def tile_dualstreamattentionwithrotaryembedding_pb_t_kernel(
                     )
             held["qk_turned", head] = turned
 
-        def copy_queries_and_keys(head):
+        def copy_queries_and_keys(head, copy=nc.scalar.copy):
             if not 0 <= head < HEADS:
                 return
             qk = work.tile([P, 2, SEQ], BF16, name="qk")
-            nc.scalar.copy(out=qk[:], in_=held["qk_turned", head][:])
+            copy(out=qk[:], in_=held["qk_turned", head][:])
             held["qk", head] = qk
 
         def scores(unit):
@@ -287,11 +293,11 @@ def tile_dualstreamattentionwithrotaryembedding_pb_t_kernel(
                     nc.tensor.transpose(turned[:, a, u, :], words[:, u * P : (u + 1) * P], ident_f32[:])
             held["e_turned", pair] = turned
 
-        def regroup_e(pair):
+        def regroup_e(pair, copy=nc.scalar.copy):
             if not 0 <= pair < PAIRS:
                 return
             grouped = work.tile([P, 2, P, PACK], BF16, name="e_grouped", align_bytes=64)
-            nc.scalar.copy(
+            copy(
                 out=grouped[:].bitcast(F32),
                 in_=held["e_turned", pair][:].rearrange("p a u q -> p a q u"),
             )
@@ -334,16 +340,18 @@ def tile_dualstreamattentionwithrotaryembedding_pb_t_kernel(
             nc.vector.reciprocal(out=inverse[:], in_=held["row_sum", head][:])
             held["inverse", head] = inverse
 
-        def normalise(head):
+        def normalise(head, first=0, end=TILES):
             if not 0 <= head < HEADS:
                 return
             item, h = divmod(head, HEADS_PER_ITEM)
             if h == 0:
                 held["y_sb", item] = stream.tile([P, TILES, MODEL_DIM], F32, name="y_sb")
             nc.vector.tensor_tensor(
-                out=held["y_sb", item][:, :, h * HEAD_DIM : (h + 1) * HEAD_DIM],
-                in0=held["y_ps", head][:],
-                in1=held["inverse", head][:].unsqueeze(2).to_broadcast([P, TILES, HEAD_DIM]),
+                out=held["y_sb", item][:, first:end, h * HEAD_DIM : (h + 1) * HEAD_DIM],
+                in0=held["y_ps", head][:, first:end, :],
+                in1=held["inverse", head][:, first:end]
+                .unsqueeze(2)
+                .to_broadcast([P, end - first, HEAD_DIM]),
                 op=mybir.AluOpType.mult,
             )
 
@@ -351,8 +359,8 @@ def tile_dualstreamattentionwithrotaryembedding_pb_t_kernel(
         load_tokens(0)
         load_queries_and_keys(0, 1, 1)
         load_weights()
-        load_queries_and_keys(0, 2, 3)
         load_biases()
+        load_queries_and_keys(0, 2, 3)
         load_tokens(1)
         load_queries_and_keys(1)
         load_tokens(2)
@@ -360,19 +368,29 @@ def tile_dualstreamattentionwithrotaryembedding_pb_t_kernel(
 
         transpose_queries_and_keys(0)
         copy_queries_and_keys(0)
-        scores(0)
-        scores(1)
+        for unit in range(TILES):
+            scores(unit)
         row_max(0)
         row_max(1)
         shift_of(0)
-        for tile_index in range(TOKEN_LEAD):
+        row_max(2)
+        row_max(3)
+        shift_of(1)
+        for tile_index in range(2):
             transpose_tokens(tile_index)
             regroup_tokens(tile_index)
-            quantise_tokens(tile_index)
+        exponentials(0)
+        exponentials(1)
         transpose_queries_and_keys(1)
         copy_queries_and_keys(1)
+        transpose_tokens(2)
+        regroup_tokens(2)
+        transpose_tokens(3)
+        regroup_tokens(3)
+        for tile_index in range(3):
+            quantise_tokens(tile_index)
 
-        for step in range(LAST_STEP + 1):
+        for step in range(1, PAIRS - 1):
             even = step % 2 == 0
             half = step // 2
 
@@ -394,24 +412,57 @@ def tile_dualstreamattentionwithrotaryembedding_pb_t_kernel(
                 regroup_tokens(half + TOKEN_LEAD)
             else:
                 copy_queries_and_keys(half + 2)
-            if step == 1:
-                repeat_bias_of_x()
 
             row_max(2 * step + 2)
             row_max(2 * step + 3)
             shift_of(step + 1)
-            quantise_e(step - 2)
+            if step == 1:
+                interleave_biases()
             if even:
+                quantise_e(step - 2)
                 normalise(half - 3)
-                add_bias(half - 1)
+                quantise_values(half - 2)
             else:
-                quantise_values(half - 1)
+                quantise_e(step - 2)
+                add_bias(half - 1)
                 quantise_tokens(half + TOKEN_LEAD)
                 reciprocal_of_row_sums(half - 1)
 
-            if step % STEPS_PER_ITEM == 4:
-                store((step - 12) // STEPS_PER_ITEM)
+            if step % STEPS_PER_ITEM == 4 and step > STEPS_PER_ITEM:
+                store(step // STEPS_PER_ITEM - 1)
             if step % STEPS_PER_ITEM == 1:
                 load_tokens(step // STEPS_PER_ITEM + 3)
             if step % STEPS_PER_ITEM == 5:
                 load_queries_and_keys(step // STEPS_PER_ITEM + 3)
+
+        last = HEADS - 1
+        final = (HEADS_PER_ITEM - 1, HEADS_PER_ITEM)
+        transpose_e(PAIRS - 2)
+        attend(PAIRS - 6)
+        attend(PAIRS - 5)
+        add_bias(last - 1)
+        project_values(last)
+        exponentials(UNITS - 2)
+        exponentials(UNITS - 1)
+        quantise_e(PAIRS - 3)
+        quantise_values(last - 1)
+        reciprocal_of_row_sums(last - 1)
+        normalise(last - 2)
+        add_bias(last)
+        regroup_e(PAIRS - 2, nc.vector.tensor_copy)
+        quantise_values(last)
+        transpose_e(PAIRS - 1)
+        attend(PAIRS - 4)
+        attend(PAIRS - 3)
+        regroup_e(PAIRS - 1)
+        normalise(last - 1)
+        store(BATCH - 1, heads=(0, HEADS_PER_ITEM - 1))
+        quantise_e(PAIRS - 2)
+        reciprocal_of_row_sums(last)
+        attend(PAIRS - 2)
+        quantise_e(PAIRS - 1)
+        normalise(last, 0, 2)
+        store(BATCH - 1, heads=final, tiles=(0, 2))
+        attend(PAIRS - 1)
+        normalise(last, 2, TILES)
+        store(BATCH - 1, heads=final, tiles=(2, TILES))

import math
from contextlib import ExitStack

import concourse.mybir as mybir
from concourse.masks import make_identity

F32 = mybir.dt.float32
BF16 = mybir.dt.bfloat16
U32 = mybir.dt.uint32
U8 = mybir.dt.uint8
I32 = mybir.dt.int32
FP8X4 = mybir.dt.float8_e4m3fn_x4

P = 128
PACK = 4
BATCH = 12
HEADS_PER_ITEM = 4
SEQ = 512
HEAD_DIM = 128
MODEL_DIM = 512
TILES = SEQ // P
HEADS = BATCH * HEADS_PER_ITEM
UNITS = HEADS * TILES
PAIRS = UNITS // 2
TOKEN_TILES = BATCH * TILES
SCALE = 1.0 / math.sqrt(HEAD_DIM)

FLOPS = 3 * 2 * BATCH * SEQ * SEQ * MODEL_DIM

TOKEN_LEAD = TILES - 1
ATTEND_LAG = 5
STEPS_PER_ITEM = 2 * HEADS_PER_ITEM


def tile_dualstreamattentionwithrotaryembedding_pb_t_kernel(
    tc, q_rot, k_rot, x, c, Wv_x_words, Wv_x_scales, bv_x, Wv_c_words, Wv_c_scales, bv_c, out_0, out_1
):
    nc = tc.nc
    with ExitStack() as ctx:
        ctx.enter_context(tc.manual_schedule())
        const = ctx.enter_context(tc.tile_pool(name="const", bufs=1))
        stream = ctx.enter_context(tc.tile_pool(name="stream", bufs=3))
        work = ctx.enter_context(tc.tile_pool(name="work", bufs=3))
        psum_scores = ctx.enter_context(tc.psum_pool(name="psum_scores", bufs=4))
        psum_turned = ctx.enter_context(tc.psum_pool(name="psum_turned", bufs=2))
        psum_mx = ctx.enter_context(tc.psum_pool(name="psum_mx", bufs=1))

        held = {}

        ident_bf16 = const.tile([P, P], BF16, name="ident_bf16")
        make_identity(nc, ident_bf16[:])
        ident_f32 = const.tile([P, P], F32, name="ident_f32")
        make_identity(nc, ident_f32[:])

        w_codes = const.tile([P, 2, MODEL_DIM], U32, name="w_codes", align_bytes=64)
        w_scales = const.tile([P, 2, MODEL_DIM], U8, name="w_scales", align_bytes=64)
        nc.vector.memset(w_scales[:].rearrange("p s n -> p (s n)").bitcast(I32), 0)
        bias = const.tile([P, MODEL_DIM, TILES], BF16, name="bias")
        bias_rows = const.tile([P, TILES, MODEL_DIM], BF16, name="bias_rows")

        def load_weights():
            given = ((Wv_c_words, Wv_c_scales), (Wv_x_words, Wv_x_scales))
            for s, (words, scales) in enumerate(given):
                nc.sync.dma_start(
                    out=w_codes[:, s, :].bitcast(I32),
                    in_=words[0].rearrange("p n t -> p (n t)").bitcast(I32),
                )
                for quadrant in range(4):
                    nc.sync.dma_start(
                        out=w_scales[32 * quadrant : 32 * quadrant + 4, s, :].bitcast(I32),
                        in_=scales[0, 4 * quadrant : 4 * quadrant + 4, :].bitcast(I32),
                    )

        def load_biases():
            nc.sync.dma_start(out=bias_rows[:, 0, :], in_=bv_c.partition_broadcast(P))
            nc.sync.dma_start(out=bias_rows[:, 1, :], in_=bv_x.partition_broadcast(P))

        def interleave_biases():
            nc.vector.tensor_copy(
                out=bias_rows[:, 2:TILES, :],
                in_=bias_rows[:, 1:2, :].to_broadcast([P, TILES - 2, MODEL_DIM]),
            )
            nc.vector.tensor_copy(out=bias[:], in_=bias_rows[:].rearrange("p t n -> p n t"))

        def load_tokens(item):
            if not 0 <= item < BATCH:
                return
            tokens = stream.tile([P, TILES, MODEL_DIM], BF16, name="tokens")
            nc.sync.dma_start(out=tokens[:, 0, :], in_=c[item])
            nc.sync.dma_start(
                out=tokens[:, 1:TILES, :], in_=x[item].rearrange("(p t) k -> p t k", p=P)
            )
            held["tokens", item] = tokens

        def load_queries_and_keys(item, first_head=0, last_head=HEADS_PER_ITEM - 1):
            if not 0 <= item < BATCH:
                return
            if first_head == 0:
                for name in ("queries", "keys"):
                    held[name, item] = stream.tile(
                        [P, HEADS_PER_ITEM * TILES, HEAD_DIM], BF16, name=name
                    )
            heads = slice(first_head, last_head + 1)
            for name, source in (("queries", q_rot), ("keys", k_rot)):
                tile = held[name, item][:].rearrange("p (h t) d -> p h (t d)", t=TILES)
                nc.sync.dma_start(
                    out=tile[:, heads, 0:HEAD_DIM],
                    in_=source[item, heads, 0:P, :].rearrange("h p d -> p h d"),
                )
                nc.sync.dma_start(
                    out=tile[:, heads, HEAD_DIM:],
                    in_=source[item, heads, P:SEQ, :].rearrange("h (p t) d -> p h (t d)", p=P),
                )

        def store(item, heads=(0, HEADS_PER_ITEM), tiles=(0, TILES)):
            if not 0 <= item < BATCH:
                return
            y_sb = held["y_sb", item]
            columns = slice(heads[0] * HEAD_DIM, heads[1] * HEAD_DIM)
            if tiles[0] == 0:
                nc.sync.dma_start(out=out_1[item, :, columns], in_=y_sb[:, 0, columns])
            first = max(tiles[0], 1)
            nc.sync.dma_start(
                out=out_0[item].rearrange("(p t) n -> p t n", p=P)[:, first - 1 : tiles[1] - 1, columns],
                in_=y_sb[:, first : tiles[1], columns],
            )

        def transpose_tokens(tile_index):
            if not 0 <= tile_index < TOKEN_TILES:
                return
            item, t = divmod(tile_index, TILES)
            words = held["tokens", item][:, t, :].bitcast(F32)
            turned = psum_turned.tile([P, 2, P], F32, name="tokens_turned", tag="turned")
            for u in range(2):
                nc.tensor.transpose(turned[:, u, :], words[:, u : MODEL_DIM // 2 : 2], ident_f32[:])
            held["tokens_turned", tile_index] = turned

        def regroup_tokens(tile_index, copy=nc.scalar.copy):
            if not 0 <= tile_index < TOKEN_TILES:
                return
            grouped = work.tile([P, P, PACK], BF16, name="tokens_grouped", align_bytes=64)
            copy(
                out=grouped[:].bitcast(F32),
                in_=held["tokens_turned", tile_index][:].rearrange("p u i -> p i u"),
            )
            held["tokens_grouped", tile_index] = grouped

        def quantise_tokens(tile_index):
            if not 0 <= tile_index < TOKEN_TILES:
                return
            item, t = divmod(tile_index, TILES)
            if t == 0:
                held["x_codes", item] = work.tile([P, SEQ], U32, name="x_codes", align_bytes=64)
                held["x_scales", item] = work.tile([P, SEQ], U8, name="x_scales", align_bytes=64)
            columns = slice(t * P, (t + 1) * P)
            nc.vector.quantize_mx(
                out=held["x_codes", item][:, columns].bitcast(FP8X4),
                scales=held["x_scales", item][:, columns],
                in_=held["tokens_grouped", tile_index][:].rearrange("p i t -> p (i t)"),
            )

        def project_values(head):
            if not 0 <= head < HEADS:
                return
            item, h = divmod(head, HEADS_PER_ITEM)
            v_ps = psum_mx.tile([P, TILES, HEAD_DIM], F32, name="v_ps")
            for t in range(TILES):
                s = min(t, 1)
                nc.tensor.matmul_mx(
                    out=v_ps[:, t, :],
                    lhsT=held["x_codes", item][:, t * P : (t + 1) * P].bitcast(FP8X4),
                    lhsT_scale=held["x_scales", item][:, t * P : (t + 1) * P],
                    rhs=w_codes[:, s, h * HEAD_DIM : (h + 1) * HEAD_DIM].bitcast(FP8X4),
                    rhs_scale=w_scales[:, s, h * HEAD_DIM : (h + 1) * HEAD_DIM],
                    start=True,
                    stop=True,
                )
            held["v_ps", head] = v_ps

        def add_bias(head):
            if not 0 <= head < HEADS:
                return
            h = head % HEADS_PER_ITEM
            grouped = work.tile([P, HEAD_DIM, PACK], BF16, name="v_grouped", align_bytes=64)
            nc.vector.tensor_tensor(
                out=grouped[:],
                in0=held["v_ps", head][:].rearrange("p t d -> p d t"),
                in1=bias[:, h * HEAD_DIM : (h + 1) * HEAD_DIM, :],
                op=mybir.AluOpType.add,
            )
            held["v_grouped", head] = grouped

        def quantise_values(head):
            if not 0 <= head < HEADS:
                return
            v_codes = work.tile([P, HEAD_DIM], U32, name="v_codes", align_bytes=64)
            v_scales = work.tile([P, HEAD_DIM], U8, name="v_scales", align_bytes=64)
            nc.vector.quantize_mx(
                out=v_codes[:].bitcast(FP8X4),
                scales=v_scales[:],
                in_=held["v_grouped", head][:].rearrange("p d t -> p (d t)"),
            )
            held["v_codes", head] = v_codes
            held["v_scales", head] = v_scales

        def transpose_queries_and_keys(head):
            if not 0 <= head < HEADS:
                return
            item, h = divmod(head, HEADS_PER_ITEM)
            turned = psum_turned.tile([P, 2, SEQ], BF16, name="qk_turned", tag="turned")
            for side, name in enumerate(("queries", "keys")):
                for t in range(TILES):
                    nc.tensor.transpose(
                        turned[:, side, t * P : (t + 1) * P],
                        held[name, item][:, h * TILES + t, :],
                        ident_bf16[:],
                    )
            held["qk_turned", head] = turned

        def copy_queries_and_keys(head, copy=nc.scalar.copy):
            if not 0 <= head < HEADS:
                return
            qk = work.tile([P, 2, SEQ], BF16, name="qk")
            copy(out=qk[:], in_=held["qk_turned", head][:])
            held["qk", head] = qk

        def scores(unit):
            if not 0 <= unit < UNITS:
                return
            head, i = divmod(unit, TILES)
            s_ps = psum_scores.tile([P, SEQ], F32, name="s_ps")
            nc.tensor.matmul(
                out=s_ps[:],
                lhsT=held["qk", head][:, 0, i * P : (i + 1) * P],
                rhs=held["qk", head][:, 1, :],
                start=True,
                stop=True,
            )
            held["s_ps", unit] = s_ps

        def row_max(unit):
            if not 0 <= unit < UNITS:
                return
            pair, a = divmod(unit, 2)
            if a == 0:
                held["row_max", pair] = work.tile([P, 2], F32, name="row_max")
            nc.vector.tensor_reduce(
                out=held["row_max", pair][:, a : a + 1],
                in_=held["s_ps", unit][:],
                axis=mybir.AxisListType.X,
                op=mybir.AluOpType.max,
            )

        def shift_of(pair):
            if not 0 <= pair < PAIRS:
                return
            shift = work.tile([P, 2], F32, name="shift")
            nc.gpsimd.tensor_scalar(
                out=shift[:],
                in0=held["row_max", pair][:],
                scalar1=-SCALE,
                scalar2=0.0,
                op0=mybir.AluOpType.mult,
                op1=mybir.AluOpType.add,
            )
            held["shift", pair] = shift

        def exponentials(unit):
            if not 0 <= unit < UNITS:
                return
            pair, a = divmod(unit, 2)
            head, i = divmod(unit, TILES)
            if a == 0:
                held["e", pair] = work.tile([P, 2, SEQ], BF16, name="e")
            if i == 0:
                held["row_sum", head] = work.tile([P, TILES], F32, name="row_sum")
            nc.scalar.activation(
                out=held["e", pair][:, a, :].rearrange("q (u p j) -> q u p j", u=2, j=2),
                in_=held["s_ps", unit][:].rearrange("q (u j p) -> q u p j", u=2, j=2),
                func=mybir.ActivationFunctionType.Exp,
                bias=held["shift", pair][:, a : a + 1],
                scale=SCALE,
                accum_out=held["row_sum", head][:, i : i + 1],
            )

        def transpose_e(pair):
            if not 0 <= pair < PAIRS:
                return
            turned = psum_turned.tile([P, 2, 2, P], F32, name="e_turned", tag="turned")
            for a in range(2):
                words = held["e", pair][:, a, :].bitcast(F32)
                for u in range(2):
                    nc.tensor.transpose(turned[:, a, u, :], words[:, u * P : (u + 1) * P], ident_f32[:])
            held["e_turned", pair] = turned

        def regroup_e(pair, copy=nc.scalar.copy):
            if not 0 <= pair < PAIRS:
                return
            grouped = work.tile([P, 2, P, PACK], BF16, name="e_grouped", align_bytes=64)
            copy(
                out=grouped[:].bitcast(F32),
                in_=held["e_turned", pair][:].rearrange("p a u q -> p a q u"),
            )
            held["e_grouped", pair] = grouped

        def quantise_e(pair):
            if not 0 <= pair < PAIRS:
                return
            e_codes = work.tile([P, 2 * P], U32, name="e_codes", align_bytes=64, bufs=ATTEND_LAG)
            e_scales = work.tile([P, 2 * P], U8, name="e_scales", align_bytes=64, bufs=ATTEND_LAG)
            nc.vector.quantize_mx(
                out=e_codes[:].bitcast(FP8X4),
                scales=e_scales[:],
                in_=held["e_grouped", pair][:].rearrange("p a q t -> p (a q t)"),
            )
            held["e_codes", pair] = e_codes
            held["e_scales", pair] = e_scales

        def attend(pair):
            if not 0 <= pair < PAIRS:
                return
            head, half = divmod(pair, 2)
            if half == 0:
                held["y_ps", head] = psum_mx.tile([P, TILES, HEAD_DIM], F32, name="y_ps")
            for a in range(2):
                nc.tensor.matmul_mx(
                    out=held["y_ps", head][:, 2 * half + a, :],
                    lhsT=held["e_codes", pair][:, a * P : (a + 1) * P].bitcast(FP8X4),
                    lhsT_scale=held["e_scales", pair][:, a * P : (a + 1) * P],
                    rhs=held["v_codes", head][:].bitcast(FP8X4),
                    rhs_scale=held["v_scales", head][:],
                    start=True,
                    stop=True,
                )

        def reciprocal_of_row_sums(head):
            if not 0 <= head < HEADS:
                return
            inverse = work.tile([P, TILES], F32, name="inverse")
            nc.vector.reciprocal(out=inverse[:], in_=held["row_sum", head][:])
            held["inverse", head] = inverse

        def normalise(head, first=0, end=TILES):
            if not 0 <= head < HEADS:
                return
            item, h = divmod(head, HEADS_PER_ITEM)
            if h == 0:
                held["y_sb", item] = stream.tile([P, TILES, MODEL_DIM], F32, name="y_sb")
            nc.vector.tensor_tensor(
                out=held["y_sb", item][:, first:end, h * HEAD_DIM : (h + 1) * HEAD_DIM],
                in0=held["y_ps", head][:, first:end, :],
                in1=held["inverse", head][:, first:end]
                .unsqueeze(2)
                .to_broadcast([P, end - first, HEAD_DIM]),
                op=mybir.AluOpType.mult,
            )

        load_queries_and_keys(0, 0, 0)
        load_tokens(0)
        load_queries_and_keys(0, 1, 1)
        load_weights()
        load_biases()
        load_queries_and_keys(0, 2, 3)
        load_tokens(1)
        load_queries_and_keys(1)
        load_tokens(2)
        load_queries_and_keys(2)

        transpose_queries_and_keys(0)
        copy_queries_and_keys(0)
        for unit in range(TILES):
            scores(unit)
        row_max(0)
        row_max(1)
        shift_of(0)
        row_max(2)
        row_max(3)
        shift_of(1)
        for tile_index in range(2):
            transpose_tokens(tile_index)
            regroup_tokens(tile_index)
        exponentials(0)
        exponentials(1)
        transpose_queries_and_keys(1)
        copy_queries_and_keys(1)
        transpose_tokens(2)
        regroup_tokens(2)
        transpose_tokens(3)
        regroup_tokens(3)
        for tile_index in range(3):
            quantise_tokens(tile_index)

        for step in range(1, PAIRS - 1):
            even = step % 2 == 0
            half = step // 2

            scores(2 * step + 2)
            scores(2 * step + 3)
            transpose_e(step - 1)
            if even:
                transpose_tokens(half + TOKEN_LEAD)
            else:
                transpose_queries_and_keys(half + 2)
            attend(step - ATTEND_LAG)
            if even:
                project_values(half - 1)

            exponentials(2 * step)
            exponentials(2 * step + 1)
            regroup_e(step - 1)
            if even:
                regroup_tokens(half + TOKEN_LEAD)
            else:
                copy_queries_and_keys(half + 2)

            row_max(2 * step + 2)
            row_max(2 * step + 3)
            shift_of(step + 1)
            if step == 1:
                interleave_biases()
            if even:
                quantise_e(step - 2)
                normalise(half - 3)
                quantise_values(half - 2)
            else:
                quantise_e(step - 2)
                add_bias(half - 1)
                quantise_tokens(half + TOKEN_LEAD)
                reciprocal_of_row_sums(half - 1)

            if step % STEPS_PER_ITEM == 4 and step > STEPS_PER_ITEM:
                store(step // STEPS_PER_ITEM - 1)
            if step % STEPS_PER_ITEM == 1:
                load_tokens(step // STEPS_PER_ITEM + 3)
            if step % STEPS_PER_ITEM == 5:
                load_queries_and_keys(step // STEPS_PER_ITEM + 3)

        last = HEADS - 1
        final = (HEADS_PER_ITEM - 1, HEADS_PER_ITEM)
        transpose_e(PAIRS - 2)
        attend(PAIRS - 6)
        attend(PAIRS - 5)
        add_bias(last - 1)
        project_values(last)
        exponentials(UNITS - 2)
        exponentials(UNITS - 1)
        quantise_e(PAIRS - 3)
        quantise_values(last - 1)
        reciprocal_of_row_sums(last - 1)
        normalise(last - 2)
        add_bias(last)
        regroup_e(PAIRS - 2, nc.vector.tensor_copy)
        quantise_values(last)
        transpose_e(PAIRS - 1)
        attend(PAIRS - 4)
        attend(PAIRS - 3)
        regroup_e(PAIRS - 1)
        normalise(last - 1)
        store(BATCH - 1, heads=(0, HEADS_PER_ITEM - 1))
        quantise_e(PAIRS - 2)
        reciprocal_of_row_sums(last)
        attend(PAIRS - 2)
        quantise_e(PAIRS - 1)
        normalise(last, 0, 2)
        store(BATCH - 1, heads=final, tiles=(0, 2))
        attend(PAIRS - 1)
        normalise(last, 2, TILES)
        store(BATCH - 1, heads=final, tiles=(2, TILES))
